import numpy as np
import ml_dtypes


def mxq(x, axis, fmt="e4m3"):
    dtype, down = {"e4m3": (ml_dtypes.float8_e4m3fn, 7), "e5m2": (ml_dtypes.float8_e5m2, 14)}[fmt]
    v = np.moveaxis(np.asarray(x, np.float32).astype(ml_dtypes.bfloat16).astype(np.float64), axis, -1)
    blocks = v.reshape(v.shape[:-1] + (-1, 32))
    amax = np.abs(blocks).max(-1, keepdims=True)
    byte = np.maximum(np.where(amax > 0, np.frexp(amax)[1] - 1 + 127, 0) - down, 1)
    scale = np.exp2(byte - 127.0)
    codes = (blocks / scale).astype(np.float32).astype(dtype).astype(np.float64)
    return np.moveaxis((codes * scale).reshape(v.shape), -1, axis)


WIDE = False


def mx_kscale(k):
    if not WIDE:
        return np.ones(k)
    levels = np.array([18, -18])
    if k % 512:
        return np.exp2(np.random.permutation(np.resize(levels, k // 32))).repeat(32)
    a = np.empty((k // 512, 16))
    for p in range(k // 512):
        a[p, :8] = np.random.permutation(np.resize(levels, 8))
        for g in range(8):
            far = levels[np.abs(levels - a[p, g]) >= 10]
            a[p, g + 8] = far[np.random.randint(len(far))]
    return np.exp2(a.ravel()).repeat(32)


BF16 = ml_dtypes.bfloat16


def bf(x):
    return np.asarray(x, np.float32).astype(BF16)


def f64(x):
    return np.asarray(x).astype(np.float64)


B, S, DIM, H, HKV, HD, RD, TRAIN_SEQ = 4, 256, 1024, 8, 4, 128, 64, 128
E, EKV, HALF = H * HD, HKV * HD, RD // 2
T, J = B * S, E + 2 * EKV
BASE = 10000.0
EPS = 1.1920929e-07


def rope_tables():
    if S > TRAIN_SEQ:
        base = BASE * (S / TRAIN_SEQ) ** (RD / (RD - 2))
    else:
        base = BASE
    inv_freq = 1.0 / base ** (np.arange(0, RD, 2) / RD)
    freqs = np.outer(np.arange(S), inv_freq)
    return np.cos(freqs), np.sin(freqs)


def rope_backward(g, cos, sin):
    c = cos[None, :, None, :]
    sn = sin[None, :, None, :]
    g1, g2, g_pass = g[..., :HALF], g[..., HALF:RD], g[..., RD:]
    return np.concatenate([g1 * c - g2 * sn, g1 * sn + g2 * c, g_pass], axis=-1)


def rms_norm_backward(dn, u):
    r = 1.0 / np.sqrt(np.mean(np.square(u), axis=-1, keepdims=True) + EPS)
    n = u * r
    return r * (dn - n * np.mean(dn * n, axis=-1, keepdims=True))


def draw_grad(heads):
    return np.random.standard_normal((B, S, heads, HD)) * np.exp2(np.random.randint(-6, 1, (B, S, 1, 1)))


def setup_inputs():
    s = mx_kscale(T).reshape(B, S, 1)
    u = mx_kscale(J)
    h = np.arange(H + HKV)
    uh = np.repeat(u[HD * h + 32 * (h % 4)], HD)
    uq, uk, uv = uh[:E], uh[E:], u[E + EKV:]
    c, sn = rope_tables()
    x0 = bf(np.random.standard_normal((B, S, DIM)))
    wq0 = bf(np.random.standard_normal((E, DIM)) / np.sqrt(DIM))
    wk0 = bf(np.random.standard_normal((EKV, DIM)) / np.sqrt(DIM))
    wv0 = bf(np.random.standard_normal((EKV, DIM)) / np.sqrt(DIM))
    q_gain = bf(1.0 + 0.1 * np.random.standard_normal(H))
    q0 = (f64(x0) @ f64(wq0).T).reshape(B, S, H, HD)
    k0 = (f64(x0) @ f64(wk0).T).reshape(B, S, HKV, HD)
    s4 = s[..., None]
    g0 = bf(draw_grad(H) / s4 * uq.reshape(H, HD))
    g1 = bf(draw_grad(HKV) / s4 * uk.reshape(HKV, HD))
    g2 = bf(draw_grad(HKV) / s4 * uv.reshape(HKV, HD))
    return {"x": bf(f64(x0) * s),
            "Wq": bf(f64(wq0) / uq[:, None]),
            "Wk": bf(f64(wk0) / uk[:, None]),
            "Wv": bf(f64(wv0) / uv[:, None]),
            "q_gain": q_gain,
            "cos_tab": bf(c), "sin_tab": bf(sn),
            "q0": np.asarray(q0, np.float32), "k0": np.asarray(k0, np.float32),
            "grad_0": g0, "grad_1": g1, "grad_2": g2}


def reference(x, Wq, Wk, Wv, q_gain, cos_tab, sin_tab, q0, k0, grad_0, grad_1, grad_2):
    c, sn = f64(cos_tab), f64(sin_tab)
    dq = rms_norm_backward(rope_backward(f64(grad_0) * f64(q_gain)[None, None, :, None], c, sn), f64(q0))
    dk = rms_norm_backward(rope_backward(f64(grad_1), c, sn), f64(k0))
    dv = f64(grad_2)
    dz = np.concatenate([dq.reshape(T, E), dk.reshape(T, EKV), dv.reshape(T, EKV)], axis=1)
    w = np.concatenate([f64(Wq), f64(Wk), f64(Wv)], axis=0)
    dx = mxq(dz, 1, "e5m2") @ mxq(w, 0, "e4m3")
    xt = mxq(f64(x).reshape(T, DIM), 0, "e4m3")
    dw = mxq(dz, 0, "e5m2").T @ xt
    return dx.reshape(B, S, DIM), dw[:E], dw[E:E + EKV], dw[E + EKV:]

@@ -1,0 +1,476 @@
+from contextlib import ExitStack
+
+import concourse.mybir as mybir
+from concourse.masks import make_identity
+
+FLOPS = 2 * 2 * 1024 * 2048 * 1024
+
+F32 = mybir.dt.float32
+BF16 = mybir.dt.bfloat16
+U32 = mybir.dt.uint32
+U8 = mybir.dt.uint8
+E4M3 = mybir.dt.float8_e4m3fn_x4
+E5M2 = mybir.dt.float8_e5m2_x4
+ALU = mybir.AluOpType
+ACT = mybir.ActivationFunctionType
+
+P = 128
+PACK = 4
+DIM = 1024
+CH = 512
+HEADS = 4
+HD = 128
+HALF = 32
+EPS = 1.1920929e-07
+C_Q0, C_Q1, C_K, C_V = range(4)
+
+
+def tile_causalselfattention_pa_v_kernel(
+    tc, x, Wq, Wk, Wv, q_gain, cos_tab, sin_tab, q0, k0, grad_0, grad_1, grad_2, out_0, out_1, out_2, out_3
+):
+    nc = tc.nc
+    x2 = x.rearrange("b s d -> (b s) d")
+    u2 = {C_Q0: q0.rearrange("b s h d -> (b s) (h d)"), C_K: k0.rearrange("b s h d -> (b s) (h d)")}
+    u2[C_Q1] = u2[C_Q0]
+    g2 = {C_Q0: grad_0.rearrange("b s h d -> (b s) (h d)"), C_K: grad_1.rearrange("b s h d -> (b s) (h d)"),
+          C_V: grad_2.rearrange("b s h d -> (b s) (h d)")}
+    g2[C_Q1] = g2[C_Q0]
+    first_col = {C_Q0: 0, C_Q1: CH, C_K: 0, C_V: 0}
+    w_rows = {C_Q0: Wq[0:CH, :], C_Q1: Wq[CH : 2 * CH, :], C_K: Wk, C_V: Wv}
+    dw_rows = {C_Q0: out_1[0:CH, :], C_Q1: out_1[CH : 2 * CH, :], C_K: out_2, C_V: out_3}
+    dx2 = out_0.rearrange("b s d -> (b s) d")
+
+    units = [(C_K, 0), (C_Q0, 0), (C_Q1, 0), (C_K, 1), (C_Q0, 1), (C_Q1, 1)]
+
+    with ExitStack() as ctx:
+        const = ctx.enter_context(tc.tile_pool(name="const", bufs=1))
+        keep = ctx.enter_context(tc.tile_pool(name="keep", bufs=1))
+        io = ctx.enter_context(tc.tile_pool(name="io", bufs=3))
+        work = ctx.enter_context(tc.tile_pool(name="work", bufs=2))
+        psum = ctx.enter_context(tc.psum_pool(name="psum", bufs=1))
+        ctx.enter_context(tc.manual_schedule())
+
+        def token_view(rows, g, c0, width):
+            return rows[g * 512 : (g + 1) * 512, c0 : c0 + width].rearrange("(p j) w -> p j w", j=PACK)
+
+        u_t, g_t, raw_t = {}, {}, {}
+
+        def load_u(e, split=False):
+            c, g = units[e]
+            u = io.tile([P, PACK, CH], F32, name="u", bufs=4)
+            view = token_view(u2[c], g, first_col[c], CH)
+            if split:
+                for j in (0, 2):
+                    nc.sync.dma_start(out=u[:, j : j + 2, :], in_=view[:, j : j + 2, :])
+            else:
+                nc.sync.dma_start(out=u[:], in_=view)
+            u_t[e] = u
+
+        def load_g(c, g):
+            t = io.tile([P, PACK, CH], BF16, name="gr", bufs=5)
+            nc.sync.dma_start(out=t[:], in_=token_view(g2[c], g, first_col[c], CH))
+            g_t[c, g] = t
+
+        def load_raw(key, rows):
+            t = io.tile([P, PACK, DIM], BF16, name="raw", bufs=3)
+            nc.sync.dma_start(out=t[:], in_=rows.rearrange("(p j) w -> p j w", j=PACK))
+            raw_t[key] = t
+
+        ident_f = const.tile([P, P], F32, name="ident_f")
+        make_identity(nc, ident_f[:])
+        ident_b = const.tile([P, P], BF16, name="ident_b")
+        make_identity(nc, ident_b[:])
+        cos_b = const.tile([P, PACK, HALF], BF16, name="cos_b")
+        sin_b = const.tile([P, PACK, HALF], BF16, name="sin_b")
+        gain_b = const.tile([P, 8], BF16, name="gain_b")
+        cos2 = const.tile([P, PACK, 2 * HALF], F32, name="cos2")
+        nsin = const.tile([P, PACK, HALF], F32, name="nsin")
+        vjunk = const.tile([P, 8, HD], BF16, name="vjunk")
+        sjunk = const.tile([P, 8, HD], BF16, name="sjunk")
+
+        load_u(0, split=True)
+        load_g(*units[0])
+        for half in range(2):
+            rows = slice(64 * half, 64 * half + 64)
+            nc.sync.dma_start(out=cos_b[rows], in_=cos_tab.rearrange("(p j) w -> p j w", j=PACK))
+            nc.sync.dma_start(out=sin_b[rows], in_=sin_tab.rearrange("(p j) w -> p j w", j=PACK))
+        nc.sync.dma_start(out=gain_b[:], in_=q_gain.partition_broadcast(P))
+        load_g(C_V, 0)
+        load_u(1)
+        load_g(*units[1])
+        load_g(C_V, 1)
+        load_raw("x0", x2[0:512, :])
+        load_raw("x1", x2[512:1024, :])
+        load_u(2)
+        load_g(*units[2])
+        load_raw("w3", w_rows[C_V])
+        dz_t = {(C_V, 0): g_t[C_V, 0], (C_V, 1): g_t[C_V, 1]}
+        def tables():
+            nc.scalar.copy(out=cos2[:, :, 0:HALF], in_=cos_b[:])
+            nc.scalar.copy(out=cos2[:, :, HALF : 2 * HALF], in_=cos_b[:])
+            nc.gpsimd.tensor_scalar(out=nsin[:], in0=sin_b[:], scalar1=-1.0, scalar2=0.0, op0=ALU.mult, op1=ALU.add)
+
+        zf_codes = keep.tile([P, 8, CH], U32, name="zf_codes", align_bytes=64)
+        zf_scales = keep.tile([P, 8, CH], U8, name="zf_scales", align_bytes=64)
+        x_codes = keep.tile([P, 2, DIM], U32, name="x_codes", align_bytes=64)
+        x_scales = keep.tile([P, 2, DIM], U8, name="x_scales", align_bytes=64)
+        w_codes = keep.tile([P, 4, DIM], U32, name="w_codes", align_bytes=64)
+        w_scales = keep.tile([P, 4, DIM], U8, name="w_scales", align_bytes=64)
+        zt = {}
+
+        ss_t, std_t, r_t, a_t, nr_t, d_t, y_t, nb_t = {}, {}, {}, {}, {}, {}, {}, {}
+
+        def squares(e, on_vector=()):
+            ss = work.tile([P, 16], F32, name="ss", bufs=2)
+            for j in range(PACK):
+                for h in range(HEADS):
+                    i = j * HEADS + h
+                    src = u_t[e][:, j, h * HD : (h + 1) * HD]
+                    if j in on_vector:
+                        nc.vector.scalar_tensor_tensor(out=vjunk[:, i % 8, :], in0=src, scalar=1.0, in1=src,
+                                                       op0=ALU.mult, op1=ALU.mult, accum_out=ss[:, i : i + 1])
+                    else:
+                        nc.scalar.activation(out=sjunk[:, i % 8, :], in_=src, func=ACT.Square, accum_out=ss[:, i : i + 1])
+            var = work.tile([P, 16], F32, name="var", bufs=2)
+            nc.gpsimd.tensor_scalar(out=var[:], in0=ss[:], scalar1=1.0 / HD, scalar2=EPS, op0=ALU.mult, op1=ALU.add)
+            ss_t[e] = var
+
+        def root(e):
+            std = work.tile([P, 16], F32, name="std", bufs=2)
+            nc.scalar.activation(out=std[:], in_=ss_t[e][:], func=ACT.Sqrt)
+            std_t[e] = std
+
+        def factors(e):
+            c, g = units[e]
+            r = work.tile([P, 16], F32, name="r", bufs=3)
+            nc.vector.reciprocal(out=r[:], in_=std_t[e][:])
+            if c == C_K:
+                a_t[e] = r
+            else:
+                a = work.tile([P, 16], F32, name="a", bufs=3)
+                h0 = HEADS * c
+                nc.gpsimd.tensor_tensor(
+                    out=a[:].rearrange("p (j h) -> p j h", h=HEADS), in0=r[:].rearrange("p (j h) -> p j h", h=HEADS),
+                    in1=gain_b[:, h0 : h0 + HEADS].unsqueeze(1).to_broadcast([P, PACK, HEADS]), op=ALU.mult)
+                a_t[e] = a
+            rr = work.tile([P, 16], F32, name="rr", bufs=2)
+            nc.gpsimd.tensor_tensor(out=rr[:], in0=r[:], in1=r[:], op=ALU.mult)
+            nr = work.tile([P, 16], F32, name="nr", bufs=3)
+            nc.gpsimd.tensor_scalar(out=nr[:], in0=rr[:], scalar1=-1.0 / HD, scalar2=0.0, op0=ALU.mult, op1=ALU.add)
+            nr_t[e] = nr
+
+        def scale(e, slots=range(PACK), on_vector=()):
+            if e not in d_t:
+                d_t[e] = work.tile([P, PACK, CH], F32, name="d", bufs=2)
+            for j in slots:
+                for h in range(HEADS):
+                    i = j * HEADS + h
+                    cols = slice(h * HD, (h + 1) * HD)
+                    if j in on_vector:
+                        nc.vector.tensor_scalar(out=d_t[e][:, j, cols], in0=g_t[units[e]][:, j, cols],
+                                                scalar1=a_t[e][:, i : i + 1], scalar2=None, op0=ALU.mult)
+                    else:
+                        nc.scalar.activation(out=d_t[e][:, j, cols], in_=g_t[units[e]][:, j, cols], func=ACT.Copy,
+                                             scale=a_t[e][:, i : i + 1])
+
+        def heads(d):
+            return d[:].rearrange("p j (h f) -> p j h f", f=HD)
+
+        def rotate_products(e, j0=0, j1=PACK):
+            d = heads(d_t[e])[:, j0:j1]
+            if e not in y_t:
+                y_t[e] = work.tile([P, PACK, HEADS, 2 * HALF], F32, name="y", bufs=1)
+            y = y_t[e][:, j0:j1]
+            full = [P, j1 - j0, HEADS, HALF]
+            nc.vector.tensor_tensor(out=y[:, :, :, 0:HALF], in0=d[:, :, :, HALF : 2 * HALF],
+                                    in1=nsin[:, j0:j1].unsqueeze(2).to_broadcast(full), op=ALU.mult)
+            nc.vector.tensor_tensor(out=y[:, :, :, HALF : 2 * HALF], in0=d[:, :, :, 0:HALF],
+                                    in1=sin_b[:, j0:j1].unsqueeze(2).to_broadcast(full), op=ALU.mult)
+            nc.vector.tensor_tensor(out=d[:, :, :, 0 : 2 * HALF], in0=d[:, :, :, 0 : 2 * HALF],
+                                    in1=cos2[:, j0:j1].unsqueeze(2).to_broadcast([P, j1 - j0, HEADS, 2 * HALF]), op=ALU.mult)
+
+        def rotate_sum(e, j0=0, j1=PACK):
+            d = heads(d_t[e])[:, j0:j1, :, 0 : 2 * HALF]
+            nc.vector.tensor_tensor(out=d, in0=d, in1=y_t[e][:, j0:j1], op=ALU.add)
+
+        def dots(e, slots=range(PACK)):
+            if e not in nb_t:
+                nb_t[e] = work.tile([P, 16], F32, name="nb", bufs=2)
+            nb = nb_t[e]
+            for j in slots:
+                for h in range(HEADS):
+                    i = j * HEADS + h
+                    cols = slice(h * HD, (h + 1) * HD)
+                    nc.vector.scalar_tensor_tensor(
+                        out=vjunk[:, i % 8, :], in0=d_t[e][:, j, cols], scalar=nr_t[e][:, i : i + 1],
+                        in1=u_t[e][:, j, cols], op0=ALU.mult, op1=ALU.mult, accum_out=nb[:, i : i + 1])
+
+        def finish(e, slots=range(PACK)):
+            key = units[e]
+            if key not in dz_t:
+                dz_t[key] = work.tile([P, PACK, CH], BF16, name="dz", bufs=2)
+            for j in slots:
+                for h in range(HEADS):
+                    i = j * HEADS + h
+                    cols = slice(h * HD, (h + 1) * HD)
+                    nc.vector.scalar_tensor_tensor(
+                        out=dz_t[key][:, j, cols], in0=u_t[e][:, j, cols], scalar=nb_t[e][:, i : i + 1],
+                        in1=d_t[e][:, j, cols], op0=ALU.mult, op1=ALU.add)
+
+        zi_t, zf_t, zt, xt_t = {}, {}, {}, {}
+
+        def token_interleave(key, c0, c1, engine="v"):
+            if c1 == c0:
+                return
+            if key not in zi_t:
+                zi_t[key] = work.tile([P, CH, PACK], BF16, name="zi", align_bytes=64, bufs=2)
+            dst = zi_t[key][:, c0:c1, :].rearrange("p (c i) t -> p c t i", i=4)
+            src = dz_t[key][:, :, c0:c1].rearrange("p t (c i) -> p c t i", i=4)
+            if engine == "s":
+                nc.scalar.copy(out=dst, in_=src)
+            else:
+                nc.vector.tensor_copy(out=dst, in_=src)
+
+        def token_quantize(key, c0=0, c1=CH):
+            if key not in zt:
+                zt[key] = (work.tile([P, CH], U32, name="zt_codes", align_bytes=64, bufs=6),
+                           work.tile([P, CH], U8, name="zt_scales", align_bytes=64, bufs=6))
+            codes, scales = zt[key]
+            nc.vector.quantize_mx(out=codes[:, c0:c1].bitcast(E5M2), scales=scales[:, c0:c1],
+                                  in_=zi_t[key][:, c0:c1, :].rearrange("p n t -> p (n t)"))
+
+        def bank(i, shape, dtype):
+            return psum.tile(shape, dtype, name="bank%d" % i, tag="bank%d" % i)
+
+        def transposes(key, slots=range(PACK)):
+            words = dz_t[key][:].rearrange("p j f -> p (j f)").bitcast(F32)
+            for j in slots:
+                if j % 2 == 0:
+                    xt_t[key, j // 2] = bank(j // 2, [P, 2, 2, P], F32)
+                for u in range(2):
+                    nc.tensor.transpose(xt_t[key, j // 2][:, j % 2, u, :],
+                                        words[:, 256 * j + u : 256 * (j + 1) : 2], ident_f[:])
+
+        def feature_copy(key, slots=range(PACK)):
+            if key not in zf_t:
+                zf_t[key] = work.tile([P, CH, PACK], BF16, name="zf", align_bytes=64, bufs=2)
+            zfw = zf_t[key][:].rearrange("p n t -> p (n t)").bitcast(F32).rearrange("p (j r u) -> p j r u", j=PACK, u=2)
+            for b in range(2):
+                js = [j for j in slots if j // 2 == b]
+                if js:
+                    nc.scalar.copy(out=zfw[:, js[0] : js[-1] + 1, :, :],
+                                   in_=xt_t[key, b][:, js[0] - 2 * b : js[-1] + 1 - 2 * b].rearrange("p j u r -> p j r u"))
+
+        def feature_quantize(key, j0=0, j1=PACK):
+            c, g = key
+            s = 4 * g + c
+            cols = slice(P * j0, P * j1)
+            nc.vector.quantize_mx(out=zf_codes[:, s, cols].bitcast(E5M2), scales=zf_scales[:, s, cols],
+                                  in_=zf_t[key][:, cols, :].rearrange("p n t -> p (n t)"))
+
+        xi_t = {}
+
+        def raw_interleave(key, parts):
+            if key not in xi_t:
+                xi_t[key] = work.tile([P, DIM * PACK], BF16, name="xi", align_bytes=64, bufs=2)
+            for i in parts:
+                ps = bank(2 + i % 2, [P, 1024], BF16)
+                for hh in range(2):
+                    w0 = 256 * i + 128 * hh
+                    nc.tensor.matmul(ps[:, 512 * hh : 512 * (hh + 1)].rearrange("p (w j) -> p w j", j=PACK), ident_b[:],
+                                     raw_t[key][:, :, w0 : w0 + 128].rearrange("p j w -> p w j"), start=True, stop=True)
+                nc.scalar.copy(out=xi_t[key][:, 1024 * i : 1024 * (i + 1)], in_=ps[:])
+
+        def raw_quantize(key):
+            codes, scales = (x_codes, x_scales) if key[0] == "x" else (w_codes, w_scales)
+            s = int(key[1])
+            nc.vector.quantize_mx(out=codes[:, s, :].bitcast(E4M3), scales=scales[:, s, :], in_=xi_t[key][:])
+
+        def evacuate(acc, dst, engine):
+            if engine == "s":
+                nc.scalar.copy(out=dst, in_=acc)
+            else:
+                nc.vector.tensor_copy(out=dst, in_=acc)
+
+        def weight_mm(c, m, n, g, acc):
+            codes, scales = zt[c, g]
+            nc.tensor.matmul_mx(out=acc[:], lhsT=codes[:, m * P : (m + 1) * P].bitcast(E5M2),
+                                lhsT_scale=scales[:, m * P : (m + 1) * P],
+                                rhs=x_codes[:, g, 512 * n : 512 * (n + 1)].bitcast(E4M3),
+                                rhs_scale=x_scales[:, g, 512 * n : 512 * (n + 1)], start=(g == 0), stop=(g == 1))
+
+        def weight_grad(c, m, banks, engines):
+            o = io.tile([P, DIM], F32, name="o", bufs=6)
+            for n in range(2):
+                acc = bank(banks[n], [P, 512], F32)
+                for g in range(2):
+                    weight_mm(c, m, n, g, acc)
+                evacuate(acc[:], o[:, 512 * n : 512 * (n + 1)], engines[n])
+            nc.sync.dma_start(out=dw_rows[c][m * P : (m + 1) * P, :], in_=o[:])
+
+        order = [C_V, C_K, C_Q0, C_Q1]
+        acc_t = {}
+
+        def data_mm(g, j, n, passes):
+            for i in passes:
+                c = order[i]
+                s = 4 * g + c
+                nc.tensor.matmul_mx(out=acc_t[g, j, n][:], lhsT=zf_codes[:, s, j * P : (j + 1) * P].bitcast(E5M2),
+                                    lhsT_scale=zf_scales[:, s, j * P : (j + 1) * P],
+                                    rhs=w_codes[:, c, 512 * n : 512 * (n + 1)].bitcast(E4M3),
+                                    rhs_scale=w_scales[:, c, 512 * n : 512 * (n + 1)],
+                                    start=(i == 0), stop=(i == 3))
+
+        def data_open(g, j, banks, passes):
+            for n in range(2):
+                acc_t[g, j, n] = bank(banks[n], [P, 512], F32)
+                data_mm(g, j, n, passes)
+
+        def data_close(g, j, passes, engines):
+            o = io.tile([P, DIM], F32, name="o", bufs=6)
+            for n in range(2):
+                data_mm(g, j, n, passes)
+                evacuate(acc_t[g, j, n][:], o[:, 512 * n : 512 * (n + 1)], engines[n])
+            nc.sync.dma_start(out=token_view(dx2, g, 0, DIM)[:, j, :], in_=o[:])
+
+        V0, V1 = (C_V, 0), (C_V, 1)
+        squares(0, on_vector=(2, 3))
+        root(0)
+        transposes(V0)
+        factors(0)
+        scale(0, [0, 1], on_vector=(0, 1))
+        tables()
+        scale(0, [2, 3])
+        rotate_products(0, 0, 2)
+        token_interleave(V0, 0, CH)
+        rotate_sum(0, 0, 2)
+        rotate_products(0, 2, 4)
+        token_quantize(V0)
+        rotate_sum(0, 2, 4)
+        feature_copy(V0)
+        squares(1)
+        root(1)
+        transposes(V1)
+        raw_interleave("x0", [0, 1])
+        feature_copy(V1)
+        dots(0)
+        factors(1)
+        feature_quantize(V0)
+        token_interleave(V1, 0, CH)
+        scale(1)
+        raw_interleave("x0", [2, 3])
+        token_quantize(V1)
+        feature_quantize(V1)
+
+        loads = {
+            1: lambda: (load_u(3), load_g(*units[3]), load_raw("w2", w_rows[C_K])),
+            2: lambda: (load_raw("w0", w_rows[C_Q0]), load_u(4), load_g(*units[4]), load_raw("w1", w_rows[C_Q1])),
+            3: lambda: (load_u(5), load_g(*units[5])),
+        }
+
+        def step(e, first=(), middle=(), late=(), s_cols=128):
+            prev = units[e - 1]
+            if e in loads:
+                loads[e]()
+            rotate_products(e)
+            if e + 1 < 6:
+                squares(e + 1)
+                root(e + 1)
+            for f in first:
+                f()
+            finish(e - 1)
+            transposes(prev)
+            rotate_sum(e)
+            if e + 1 < 6:
+                factors(e + 1)
+            feature_copy(prev)
+            token_interleave(prev, 0, s_cols, "s")
+            token_interleave(prev, s_cols, CH)
+            for f in middle:
+                f()
+            if e + 1 < 6:
+                scale(e + 1)
+            dots(e)
+            token_quantize(prev)
+            feature_quantize(prev)
+            for f in late:
+                f()
+
+        def mv(key, parts):
+            return lambda: raw_interleave(key, parts)
+
+        def rq(key):
+            return lambda: raw_quantize(key)
+
+        def dw(c, m, banks, engines="ss"):
+            return lambda: weight_grad(c, m, banks, engines)
+
+        def dx_open(g, j, banks, passes):
+            return lambda: data_open(g, j, banks, passes)
+
+        def dx_close(g, j, passes, engines="ss"):
+            return lambda: data_close(g, j, passes, engines)
+
+        def dx(g, j, banks, engines="ss"):
+            return lambda: (data_open(g, j, banks, range(4)), data_close(g, j, [], engines))
+
+        step(1, [mv("x1", [0, 1])], [mv("x1", [2, 3])], [rq("x0"), rq("x1"), mv("w3", [0, 1])])
+        step(2, [mv("w3", [2, 3]), dw(C_V, 0, (4, 5))], [mv("w2", [0, 1]), dw(C_V, 1, (6, 7))], [rq("w3"), mv("w2", [2, 3])])
+        step(3, [mv("w0", [0, 1]), dw(C_V, 2, (4, 5))], [mv("w0", [2, 3]), dw(C_V, 3, (6, 7))],
+             [rq("w2"), rq("w0"), mv("w1", [0, 1, 2, 3]), rq("w1")])
+        step(4, [dx(0, 0, (4, 5))], [dx(0, 1, (6, 7))], [dx(0, 2, (4, 5)), dx(0, 3, (6, 7))])
+
+        last = units[5]
+        prev = units[4]
+        rotate_products(5)
+        dw(C_K, 0, (4, 5))()
+        dw(C_K, 1, (6, 7))()
+        finish(4)
+        transposes(prev)
+        rotate_sum(5)
+        feature_copy(prev)
+        token_interleave(prev, 0, 256, "s")
+        dw(C_K, 2, (4, 5))()
+        token_interleave(prev, 256, CH)
+        dots(5, [0, 1])
+        feature_quantize(prev)
+        dw(C_K, 3, (6, 7))()
+        data_open(1, 0, (2, 3), range(3))
+        finish(5, [0])
+        token_quantize(prev)
+        transposes(last, [0])
+        dots(5, [2])
+        finish(5, [1])
+        feature_copy(last, [0])
+        weight_grad(C_Q0, 0, (4, 5), "ss")
+        transposes(last, [1])
+        dots(5, [3])
+        feature_quantize(last, 0, 1)
+        finish(5, [2])
+        feature_copy(last, [1])
+        weight_grad(C_Q0, 1, (6, 7), "ss")
+        transposes(last, [2])
+        data_close(1, 0, [3], "ss")
+        data_open(1, 1, (4, 5), range(3))
+        finish(5, [3])
+        feature_copy(last, [2])
+        feature_quantize(last, 1, 2)
+        transposes(last, [3])
+        data_close(1, 1, [3], "ss")
+        feature_copy(last, [3])
+        token_interleave(last, 0, 256)
+        feature_quantize(last, 2, 3)
+        data_open(1, 2, (2, 3), range(4))
+        token_interleave(last, 256, CH)
+        data_close(1, 2, [], "ss")
+        weight_grad(C_Q0, 2, (6, 7), "ss")
+        token_quantize(last, 0, 256)
+        feature_quantize(last, 3, 4)
+        token_quantize(last, 256, CH)
+        data_open(1, 3, (4, 5), range(4))
+        data_close(1, 3, [], "sv")
+        weight_grad(C_Q0, 3, (2, 3), "sv")
+        weight_grad(C_Q1, 0, (0, 1), "sv")
+        weight_grad(C_Q1, 1, (6, 7), "sv")
+        weight_grad(C_Q1, 2, (4, 5), "sv")
+        weight_grad(C_Q1, 3, (2, 3), "sv")

@@ -57,7 +57,7 @@ def tile_causalselfattention_pa_v_kernel(
 
         def load_u(e, split=False):
             c, g = units[e]
-            u = io.tile([P, PACK, CH], F32, name="u", bufs=4)
+            u = io.tile([P, PACK, CH], F32, name="u", bufs=3)
             view = token_view(u2[c], g, first_col[c], CH)
             if split:
                 for j in (0, 2):
@@ -67,7 +67,7 @@ def tile_causalselfattention_pa_v_kernel(
             u_t[e] = u
 
         def load_g(c, g):
-            t = io.tile([P, PACK, CH], BF16, name="gr", bufs=5)
+            t = io.tile([P, PACK, CH], BF16, name="gr", bufs=4)
             nc.sync.dma_start(out=t[:], in_=token_view(g2[c], g, first_col[c], CH))
             g_t[c, g] = t
 
@@ -85,7 +85,9 @@ def tile_causalselfattention_pa_v_kernel(
         gain_b = const.tile([P, 8], BF16, name="gain_b")
         cos2 = const.tile([P, PACK, 2 * HALF], F32, name="cos2")
         nsin = const.tile([P, PACK, HALF], F32, name="nsin")
-        vjunk = const.tile([P, 8, HD], BF16, name="vjunk")
+        vjunk = const.tile([P, 2, HD], BF16, name="vjunk")
+        sel = const.tile([P, 16], F32, name="sel")
+        nc.vector.tensor_reduce(out=sel[:], in_=ident_f[:].rearrange("p (g q) -> p g q", q=8), axis=mybir.AxisListType.X, op=ALU.add)
         sjunk = const.tile([P, 8, HD], BF16, name="sjunk")
 
         load_u(0, split=True)
@@ -101,9 +103,6 @@ def tile_causalselfattention_pa_v_kernel(
         load_g(C_V, 1)
         load_raw("x0", x2[0:512, :])
         load_raw("x1", x2[512:1024, :])
-        load_u(2)
-        load_g(*units[2])
-        load_raw("w3", w_rows[C_V])
         dz_t = {(C_V, 0): g_t[C_V, 0], (C_V, 1): g_t[C_V, 1]}
         def tables():
             nc.scalar.copy(out=cos2[:, :, 0:HALF], in_=cos_b[:])
@@ -118,6 +117,9 @@ def tile_causalselfattention_pa_v_kernel(
         w_scales = keep.tile([P, 4, DIM], U8, name="w_scales", align_bytes=64)
         zt = {}
 
+        def bank(i, shape, dtype):
+            return psum.tile(shape, dtype, name="bank%d" % i, tag="bank%d" % i)
+
         ss_t, std_t, r_t, a_t, nr_t, d_t, y_t, nb_t = {}, {}, {}, {}, {}, {}, {}, {}
 
         def squares(e, on_vector=()):
@@ -127,36 +129,36 @@ def tile_causalselfattention_pa_v_kernel(
                     i = j * HEADS + h
                     src = u_t[e][:, j, h * HD : (h + 1) * HD]
                     if j in on_vector:
-                        nc.vector.scalar_tensor_tensor(out=vjunk[:, i % 8, :], in0=src, scalar=1.0, in1=src,
+                        nc.vector.scalar_tensor_tensor(out=vjunk[:, i % 2, :], in0=src, scalar=1.0, in1=src,
                                                        op0=ALU.mult, op1=ALU.mult, accum_out=ss[:, i : i + 1])
                     else:
                         nc.scalar.activation(out=sjunk[:, i % 8, :], in_=src, func=ACT.Square, accum_out=ss[:, i : i + 1])
-            var = work.tile([P, 16], F32, name="var", bufs=2)
-            nc.gpsimd.tensor_scalar(out=var[:], in0=ss[:], scalar1=1.0 / HD, scalar2=EPS, op0=ALU.mult, op1=ALU.add)
-            ss_t[e] = var
+            ss_t[e] = ss
 
         def root(e):
             std = work.tile([P, 16], F32, name="std", bufs=2)
-            nc.scalar.activation(out=std[:], in_=ss_t[e][:], func=ACT.Sqrt)
+            nc.scalar.activation(out=std[:], in_=ss_t[e][:], func=ACT.Sqrt, scale=1.0 / HD, bias=EPS)
             std_t[e] = std
+
+        def inverse(e):
+            r = work.tile([P, 16], F32, name="r", bufs=3)
+            nc.vector.reciprocal(out=r[:], in_=std_t[e][:])
+            r_t[e] = r
 
         def factors(e):
             c, g = units[e]
-            r = work.tile([P, 16], F32, name="r", bufs=3)
-            nc.vector.reciprocal(out=r[:], in_=std_t[e][:])
+            r = r_t[e]
             if c == C_K:
                 a_t[e] = r
             else:
                 a = work.tile([P, 16], F32, name="a", bufs=3)
                 h0 = HEADS * c
-                nc.gpsimd.tensor_tensor(
+                nc.vector.tensor_tensor(
                     out=a[:].rearrange("p (j h) -> p j h", h=HEADS), in0=r[:].rearrange("p (j h) -> p j h", h=HEADS),
                     in1=gain_b[:, h0 : h0 + HEADS].unsqueeze(1).to_broadcast([P, PACK, HEADS]), op=ALU.mult)
                 a_t[e] = a
-            rr = work.tile([P, 16], F32, name="rr", bufs=2)
-            nc.gpsimd.tensor_tensor(out=rr[:], in0=r[:], in1=r[:], op=ALU.mult)
             nr = work.tile([P, 16], F32, name="nr", bufs=3)
-            nc.gpsimd.tensor_scalar(out=nr[:], in0=rr[:], scalar1=-1.0 / HD, scalar2=0.0, op0=ALU.mult, op1=ALU.add)
+            nc.vector.scalar_tensor_tensor(out=nr[:], in0=r[:], scalar=-1.0 / HD, in1=r[:], op0=ALU.mult, op1=ALU.mult)
             nr_t[e] = nr
 
         def scale(e, slots=range(PACK), on_vector=()):
@@ -193,17 +195,31 @@ def tile_causalselfattention_pa_v_kernel(
             d = heads(d_t[e])[:, j0:j1, :, 0 : 2 * HALF]
             nc.vector.tensor_tensor(out=d, in0=d, in1=y_t[e][:, j0:j1], op=ALU.add)
 
-        def dots(e, slots=range(PACK)):
-            if e not in nb_t:
-                nb_t[e] = work.tile([P, 16], F32, name="nb", bufs=2)
-            nb = nb_t[e]
-            for j in slots:
-                for h in range(HEADS):
-                    i = j * HEADS + h
-                    cols = slice(h * HD, (h + 1) * HD)
-                    nc.vector.scalar_tensor_tensor(
-                        out=vjunk[:, i % 8, :], in0=d_t[e][:, j, cols], scalar=nr_t[e][:, i : i + 1],
-                        in1=u_t[e][:, j, cols], op0=ALU.mult, op1=ALU.mult, accum_out=nb[:, i : i + 1])
+        prod_t, dot_t, pt_t = {}, {}, {}
+
+        def products(e, half):
+            if e not in prod_t:
+                prod_t[e] = work.tile([P, 16, P], F32, name="prod", bufs=1)
+            s = slice(8 * half, 8 * half + 8)
+            nc.vector.tensor_tensor(out=prod_t[e][:, s, :].rearrange("p s (g q) -> p g s q", q=8),
+                                    in0=d_t[e][:].rearrange("p j (h b q) -> p (j h) b q", b=16, q=8)[:, :, s, :],
+                                    in1=u_t[e][:].rearrange("p j (h b q) -> p (j h) b q", b=16, q=8)[:, :, s, :], op=ALU.mult)
+
+        def dot_transposes(e, half):
+            if half == 1:
+                dot_t[e] = bank(0, [P, 512], F32)
+            for k in range(8 * half, 8 * half + 8):
+                nc.tensor.matmul(dot_t[e][:, 0:P], prod_t[e][:, k, :], ident_f[:], is_transpose=True,
+                                 start=(k == 8), stop=(k == 7))
+
+        def dot_copy(e):
+            pt_t[e] = work.tile([P, P], F32, name="pt", bufs=2)
+            nc.scalar.copy(out=pt_t[e][:], in_=dot_t[e][:, 0:P])
+            nc.tensor.matmul(dot_t[e][:, P : P + 16], pt_t[e][:], sel[:], start=True, stop=True)
+
+        def dot_finish(e):
+            nb_t[e] = work.tile([P, 16], F32, name="nb", bufs=2)
+            nc.vector.tensor_tensor(out=nb_t[e][:], in0=dot_t[e][:, P : P + 16], in1=nr_t[e][:], op=ALU.mult)
 
         def finish(e, slots=range(PACK)):
             key = units[e]
@@ -239,9 +255,6 @@ def tile_causalselfattention_pa_v_kernel(
             nc.vector.quantize_mx(out=codes[:, c0:c1].bitcast(E5M2), scales=scales[:, c0:c1],
                                   in_=zi_t[key][:, c0:c1, :].rearrange("p n t -> p (n t)"))
 
-        def bank(i, shape, dtype):
-            return psum.tile(shape, dtype, name="bank%d" % i, tag="bank%d" % i)
-
         def transposes(key, slots=range(PACK)):
             words = dz_t[key][:].rearrange("p j f -> p (j f)").bitcast(F32)
             for j in slots:
@@ -268,23 +281,32 @@ def tile_causalselfattention_pa_v_kernel(
             nc.vector.quantize_mx(out=zf_codes[:, s, cols].bitcast(E5M2), scales=zf_scales[:, s, cols],
                                   in_=zf_t[key][:, cols, :].rearrange("p n t -> p (n t)"))
 
-        xi_t = {}
+        xi_t, ps_t = {}, {}
+        ring = [2]
 
-        def raw_interleave(key, parts):
-            if key not in xi_t:
-                xi_t[key] = work.tile([P, DIM * PACK], BF16, name="xi", align_bytes=64, bufs=2)
-            for i in parts:
-                ps = bank(2 + i % 2, [P, 1024], BF16)
-                for hh in range(2):
-                    w0 = 256 * i + 128 * hh
-                    nc.tensor.matmul(ps[:, 512 * hh : 512 * (hh + 1)].rearrange("p (w j) -> p w j", j=PACK), ident_b[:],
-                                     raw_t[key][:, :, w0 : w0 + 128].rearrange("p j w -> p w j"), start=True, stop=True)
-                nc.scalar.copy(out=xi_t[key][:, 1024 * i : 1024 * (i + 1)], in_=ps[:])
+        def next_bank():
+            b = ring[0]
+            ring[0] = b + 1 if b < 7 else 2
+            return b
 
-        def raw_quantize(key):
+        def raw_mm(key, i):
+            ps = bank(next_bank(), [P, 1024], BF16)
+            ps_t[key, i] = ps
+            for hh in range(2):
+                w0 = 256 * i + 128 * hh
+                nc.tensor.matmul(ps[:, 512 * hh : 512 * (hh + 1)].rearrange("p (w j) -> p w j", j=PACK), ident_b[:],
+                                 raw_t[key][:, :, w0 : w0 + 128].rearrange("p j w -> p w j"), start=True, stop=True)
+
+        def raw_copy(key, i):
+            if (key, i // 2) not in xi_t:
+                xi_t[key, i // 2] = work.tile([P, 2048], BF16, name="xi", align_bytes=64, bufs=4)
+            nc.scalar.copy(out=xi_t[key, i // 2][:, 1024 * (i % 2) : 1024 * (i % 2 + 1)], in_=ps_t[key, i][:])
+
+        def raw_quantize(key, half):
             codes, scales = (x_codes, x_scales) if key[0] == "x" else (w_codes, w_scales)
             s = int(key[1])
-            nc.vector.quantize_mx(out=codes[:, s, :].bitcast(E4M3), scales=scales[:, s, :], in_=xi_t[key][:])
+            cols = slice(512 * half, 512 * half + 512)
+            nc.vector.quantize_mx(out=codes[:, s, cols].bitcast(E4M3), scales=scales[:, s, cols], in_=xi_t[key, half][:])
 
         def evacuate(acc, dst, engine):
             if engine == "s":
@@ -299,17 +321,30 @@ def tile_causalselfattention_pa_v_kernel(
                                 rhs=x_codes[:, g, 512 * n : 512 * (n + 1)].bitcast(E4M3),
                                 rhs_scale=x_scales[:, g, 512 * n : 512 * (n + 1)], start=(g == 0), stop=(g == 1))
 
-        def weight_grad(c, m, banks, engines):
-            o = io.tile([P, DIM], F32, name="o", bufs=6)
+        def weight_open(c, m, banks=None, passes=(0, 1)):
             for n in range(2):
-                acc = bank(banks[n], [P, 512], F32)
-                for g in range(2):
-                    weight_mm(c, m, n, g, acc)
-                evacuate(acc[:], o[:, 512 * n : 512 * (n + 1)], engines[n])
-            nc.sync.dma_start(out=dw_rows[c][m * P : (m + 1) * P, :], in_=o[:])
+                if (c, m, n) not in wacc_t:
+                    wacc_t[c, m, n] = bank(banks[n] if banks else next_bank(), [P, 512], F32)
+                for g in passes:
+                    weight_mm(c, m, n, g, wacc_t[c, m, n])
+
+        o_t = {}
+
+        def emit(key, n, acc, rows, engine):
+            if key not in o_t:
+                o_t[key] = io.tile([P, DIM], F32, name="o", bufs=6)
+            evacuate(acc[:], o_t[key][:, 512 * n : 512 * (n + 1)], engine)
+            if n == 1:
+                nc.sync.dma_start(out=rows, in_=o_t[key][:])
+
+        def weight_out(c, m, n, engine="s"):
+            emit((c, m), n, wacc_t[c, m, n], dw_rows[c][m * P : (m + 1) * P, :], engine)
+
+        def data_out(g, j, n, engine="s"):
+            emit(("x", g, j), n, acc_t[g, j, n], token_view(dx2, g, 0, DIM)[:, j, :], engine)
 
         order = [C_V, C_K, C_Q0, C_Q1]
-        acc_t = {}
+        acc_t, wacc_t = {}, {}
 
         def data_mm(g, j, n, passes):
             for i in passes:
@@ -323,24 +358,21 @@ def tile_causalselfattention_pa_v_kernel(
 
         def data_open(g, j, banks, passes):
             for n in range(2):
-                acc_t[g, j, n] = bank(banks[n], [P, 512], F32)
+                acc_t[g, j, n] = bank(banks[n] if banks else next_bank(), [P, 512], F32)
                 data_mm(g, j, n, passes)
-
-        def data_close(g, j, passes, engines):
-            o = io.tile([P, DIM], F32, name="o", bufs=6)
-            for n in range(2):
-                data_mm(g, j, n, passes)
-                evacuate(acc_t[g, j, n][:], o[:, 512 * n : 512 * (n + 1)], engines[n])
-            nc.sync.dma_start(out=token_view(dx2, g, 0, DIM)[:, j, :], in_=o[:])
 
         V0, V1 = (C_V, 0), (C_V, 1)
         squares(0, on_vector=(2, 3))
         root(0)
         transposes(V0)
+        inverse(0)
         factors(0)
         scale(0, [0, 1], on_vector=(0, 1))
         tables()
         scale(0, [2, 3])
+        load_u(2)
+        load_g(*units[2])
+        load_raw("w3", w_rows[C_V])
         rotate_products(0, 0, 2)
         token_interleave(V0, 0, CH)
         rotate_sum(0, 0, 2)
@@ -351,126 +383,178 @@ def tile_causalselfattention_pa_v_kernel(
         squares(1)
         root(1)
         transposes(V1)
-        raw_interleave("x0", [0, 1])
         feature_copy(V1)
-        dots(0)
+        raw_mm("x0", 0)
+        raw_mm("x0", 1)
+        inverse(1)
+        products(0, 1)
         factors(1)
+        dot_transposes(0, 1)
+        products(0, 0)
+        dot_transposes(0, 0)
+        scale(1)
         feature_quantize(V0)
         token_interleave(V1, 0, CH)
-        scale(1)
-        raw_interleave("x0", [2, 3])
+        dot_copy(0)
+        raw_mm("x0", 2)
+        raw_mm("x0", 3)
+        for i in range(4):
+            raw_copy("x0", i)
+        raw_mm("x1", 0)
+        raw_mm("x1", 1)
         token_quantize(V1)
         feature_quantize(V1)
+        dot_finish(0)
 
         loads = {
-            1: lambda: (load_u(3), load_g(*units[3]), load_raw("w2", w_rows[C_K])),
-            2: lambda: (load_raw("w0", w_rows[C_Q0]), load_u(4), load_g(*units[4]), load_raw("w1", w_rows[C_Q1])),
+            1: lambda: (load_raw("w2", w_rows[C_K]), load_u(3), load_g(*units[3]), load_raw("w0", w_rows[C_Q0])),
+            2: lambda: (load_raw("w1", w_rows[C_Q1]), load_u(4), load_g(*units[4])),
             3: lambda: (load_u(5), load_g(*units[5])),
         }
 
-        def step(e, first=(), middle=(), late=(), s_cols=128):
+        def wo(c, m):
+            return lambda: weight_open(c, m)
+
+        def do(g, j):
+            return lambda: data_open(g, j, None, range(4))
+
+        def we(c, m, n):
+            return lambda: weight_out(c, m, n)
+
+        def de(g, j, n):
+            return lambda: data_out(g, j, n)
+
+        def rm(key, *tiles):
+            return lambda: [raw_mm(key, i) for i in tiles]
+
+        def rc(key, *tiles):
+            return lambda: [raw_copy(key, i) for i in tiles]
+
+        def rq(key, half):
+            return lambda: raw_quantize(key, half)
+
+        def run(fs):
+            for f in fs:
+                f()
+
+        def step(e, pe0=(), pe1=(), pe2=(), pe3=(), s0=(), s1=(), s2=(), v0=(), v1=(), s_cols=0):
             prev = units[e - 1]
+            run(pe0)
+            finish(e - 1)
+            squares(e + 1)
+            root(e + 1)
+            run(s0)
+            transposes(prev)
+            run(pe1)
             if e in loads:
                 loads[e]()
             rotate_products(e)
-            if e + 1 < 6:
-                squares(e + 1)
-                root(e + 1)
-            for f in first:
-                f()
-            finish(e - 1)
-            transposes(prev)
-            rotate_sum(e)
-            if e + 1 < 6:
-                factors(e + 1)
+            products(e, 1)
             feature_copy(prev)
             token_interleave(prev, 0, s_cols, "s")
+            run(s1)
+            dot_transposes(e, 1)
+            run(pe2)
+            rotate_sum(e)
+            inverse(e + 1)
+            run(v0)
             token_interleave(prev, s_cols, CH)
-            for f in middle:
-                f()
-            if e + 1 < 6:
-                scale(e + 1)
-            dots(e)
-            token_quantize(prev)
+            factors(e + 1)
+            products(e, 0)
+            dot_transposes(e, 0)
+            scale(e + 1)
             feature_quantize(prev)
-            for f in late:
-                f()
+            dot_copy(e)
+            token_quantize(prev)
+            run(v1)
+            run(s2)
+            run(pe3)
+            dot_finish(e)
 
-        def mv(key, parts):
-            return lambda: raw_interleave(key, parts)
-
-        def rq(key):
-            return lambda: raw_quantize(key)
-
-        def dw(c, m, banks, engines="ss"):
-            return lambda: weight_grad(c, m, banks, engines)
-
-        def dx_open(g, j, banks, passes):
-            return lambda: data_open(g, j, banks, passes)
-
-        def dx_close(g, j, passes, engines="ss"):
-            return lambda: data_close(g, j, passes, engines)
-
-        def dx(g, j, banks, engines="ss"):
-            return lambda: (data_open(g, j, banks, range(4)), data_close(g, j, [], engines))
-
-        step(1, [mv("x1", [0, 1])], [mv("x1", [2, 3])], [rq("x0"), rq("x1"), mv("w3", [0, 1])])
-        step(2, [mv("w3", [2, 3]), dw(C_V, 0, (4, 5))], [mv("w2", [0, 1]), dw(C_V, 1, (6, 7))], [rq("w3"), mv("w2", [2, 3])])
-        step(3, [mv("w0", [0, 1]), dw(C_V, 2, (4, 5))], [mv("w0", [2, 3]), dw(C_V, 3, (6, 7))],
-             [rq("w2"), rq("w0"), mv("w1", [0, 1, 2, 3]), rq("w1")])
-        step(4, [dx(0, 0, (4, 5))], [dx(0, 1, (6, 7))], [dx(0, 2, (4, 5)), dx(0, 3, (6, 7))])
+        step(1, pe0=[rm("x1", 2, 3)], pe1=[rm("w3", 0, 1)], pe2=[rm("w3", 2, 3)], pe3=[rm("w2", 0, 1)],
+             s0=[rc("x1", 0)], s1=[rc("x1", 1, 2, 3)], s2=[rc("w3", 0, 1, 2, 3)],
+             v0=[rq("x0", 0), rq("x0", 1)], v1=[rq("x1", 0), rq("x1", 1)], s_cols=128)
+        step(2, pe0=[rm("w2", 2, 3)], pe1=[rm("w0", 0, 1)], pe2=[rm("w0", 2, 3), wo(C_V, 0)], pe3=[wo(C_V, 1), rm("w1", 0, 1)],
+             s0=[rc("w2", 0)], s1=[rc("w2", 1, 2, 3)], s2=[rc("w0", 0, 1), we(C_V, 0, 0), we(C_V, 0, 1), rc("w0", 2, 3)],
+             v0=[rq("w3", 0), rq("w3", 1)], v1=[rq("w2", 0), rq("w2", 1)], s_cols=64)
+        step(3, pe0=[rm("w1", 2, 3)], pe1=[wo(C_V, 2)], pe2=[wo(C_V, 3)], pe3=[do(0, 0)],
+             s0=[we(C_V, 1, 0), we(C_V, 1, 1)], s1=[rc("w1", 0, 1, 2, 3)], s2=[we(C_V, 2, 0), we(C_V, 2, 1), we(C_V, 3, 0), we(C_V, 3, 1)],
+             v0=[rq("w0", 0), rq("w0", 1)], v1=[rq("w1", 0), rq("w1", 1)], s_cols=0)
+        step(4, pe0=[do(0, 1)], pe1=[do(0, 2)], pe2=[do(0, 3)], pe3=[wo(C_K, 0)],
+             s0=[de(0, 0, 0)], s1=[de(0, 0, 1), de(0, 1, 0), de(0, 1, 1)], s2=[de(0, 2, 0), de(0, 2, 1), de(0, 3, 0), de(0, 3, 1)], s_cols=128)
 
         last = units[5]
         prev = units[4]
-        rotate_products(5)
-        dw(C_K, 0, (4, 5))()
-        dw(C_K, 1, (6, 7))()
         finish(4)
         transposes(prev)
-        rotate_sum(5)
+        wo(C_K, 1)()
+        token_interleave(prev, 0, 192, "s")
+        token_interleave(prev, 192, CH)
+        run([we(C_K, 0, 0), we(C_K, 0, 1)])
         feature_copy(prev)
-        token_interleave(prev, 0, 256, "s")
-        dw(C_K, 2, (4, 5))()
-        token_interleave(prev, 256, CH)
-        dots(5, [0, 1])
-        feature_quantize(prev)
-        dw(C_K, 3, (6, 7))()
-        data_open(1, 0, (2, 3), range(3))
-        finish(5, [0])
+        rotate_products(5)
         token_quantize(prev)
+        wo(C_K, 2)()
+        products(5, 1)
+        run([we(C_K, 1, 0), we(C_K, 1, 1)])
+        dot_transposes(5, 1)
+        wo(C_K, 3)()
+        rotate_sum(5)
+        run([we(C_K, 2, 0), we(C_K, 2, 1)])
+        feature_quantize(prev)
+        wo(C_Q0, 0)()
+        products(5, 0)
+        dot_transposes(5, 0)
+        run([we(C_K, 3, 0)])
+        dot_copy(5)
+        weight_out(C_K, 3, 1, "v")
+        wo(C_Q0, 1)()
+        run([we(C_Q0, 0, 0)])
+        weight_out(C_Q0, 0, 1, "v")
+        wo(C_Q0, 2)()
+        dot_finish(5)
+        finish(5, [0])
+        run([we(C_Q0, 1, 0), we(C_Q0, 1, 1)])
+        wo(C_Q0, 3)()
         transposes(last, [0])
-        dots(5, [2])
         finish(5, [1])
+        run([we(C_Q0, 2, 0)])
         feature_copy(last, [0])
-        weight_grad(C_Q0, 0, (4, 5), "ss")
+        run([we(C_Q0, 2, 1)])
+        data_open(1, 0, None, range(3))
         transposes(last, [1])
-        dots(5, [3])
         feature_quantize(last, 0, 1)
         finish(5, [2])
         feature_copy(last, [1])
-        weight_grad(C_Q0, 1, (6, 7), "ss")
+        run([we(C_Q0, 3, 0), we(C_Q0, 3, 1)])
+        data_open(1, 1, None, range(3))
         transposes(last, [2])
-        data_close(1, 0, [3], "ss")
-        data_open(1, 1, (4, 5), range(3))
         finish(5, [3])
+        data_mm(1, 0, 0, [3])
+        data_mm(1, 0, 1, [3])
         feature_copy(last, [2])
         feature_quantize(last, 1, 2)
         transposes(last, [3])
-        data_close(1, 1, [3], "ss")
+        data_mm(1, 1, 0, [3])
+        data_mm(1, 1, 1, [3])
+        run([de(1, 0, 0), de(1, 0, 1)])
         feature_copy(last, [3])
         token_interleave(last, 0, 256)
         feature_quantize(last, 2, 3)
-        data_open(1, 2, (2, 3), range(4))
+        data_open(1, 2, None, range(4))
         token_interleave(last, 256, CH)
-        data_close(1, 2, [], "ss")
-        weight_grad(C_Q0, 2, (6, 7), "ss")
-        token_quantize(last, 0, 256)
+        run([de(1, 1, 0), de(1, 1, 1)])
         feature_quantize(last, 3, 4)
+        token_quantize(last, 0, 256)
         token_quantize(last, 256, CH)
-        data_open(1, 3, (4, 5), range(4))
-        data_close(1, 3, [], "sv")
-        weight_grad(C_Q0, 3, (2, 3), "sv")
-        weight_grad(C_Q1, 0, (0, 1), "sv")
-        weight_grad(C_Q1, 1, (6, 7), "sv")
-        weight_grad(C_Q1, 2, (4, 5), "sv")
-        weight_grad(C_Q1, 3, (2, 3), "sv")
+        do(1, 3)()
+        run([de(1, 2, 0)])
+        data_out(1, 2, 1, "v")
+        wo(C_Q1, 0)()
+        run([de(1, 3, 0)])
+        data_out(1, 3, 1, "v")
+        for m in range(4):
+            if m < 3:
+                wo(C_Q1, m + 1)()
+            weight_out(C_Q1, m, 0, "s")
+            weight_out(C_Q1, m, 1, "v")

from contextlib import ExitStack

import concourse.mybir as mybir
from concourse.masks import make_identity

FLOPS = 2 * 2 * 1024 * 2048 * 1024

F32 = mybir.dt.float32
BF16 = mybir.dt.bfloat16
U32 = mybir.dt.uint32
U8 = mybir.dt.uint8
E4M3 = mybir.dt.float8_e4m3fn_x4
E5M2 = mybir.dt.float8_e5m2_x4
ALU = mybir.AluOpType
ACT = mybir.ActivationFunctionType

P = 128
PACK = 4
DIM = 1024
CH = 512
HEADS = 4
HD = 128
HALF = 32
EPS = 1.1920929e-07
C_Q0, C_Q1, C_K, C_V = range(4)


def tile_causalselfattention_pa_v_kernel(
    tc, x, Wq, Wk, Wv, q_gain, cos_tab, sin_tab, q0, k0, grad_0, grad_1, grad_2, out_0, out_1, out_2, out_3
):
    nc = tc.nc
    x2 = x.rearrange("b s d -> (b s) d")
    u2 = {C_Q0: q0.rearrange("b s h d -> (b s) (h d)"), C_K: k0.rearrange("b s h d -> (b s) (h d)")}
    u2[C_Q1] = u2[C_Q0]
    g2 = {C_Q0: grad_0.rearrange("b s h d -> (b s) (h d)"), C_K: grad_1.rearrange("b s h d -> (b s) (h d)"),
          C_V: grad_2.rearrange("b s h d -> (b s) (h d)")}
    g2[C_Q1] = g2[C_Q0]
    first_col = {C_Q0: 0, C_Q1: CH, C_K: 0, C_V: 0}
    w_rows = {C_Q0: Wq[0:CH, :], C_Q1: Wq[CH : 2 * CH, :], C_K: Wk, C_V: Wv}
    dw_rows = {C_Q0: out_1[0:CH, :], C_Q1: out_1[CH : 2 * CH, :], C_K: out_2, C_V: out_3}
    dx2 = out_0.rearrange("b s d -> (b s) d")

    units = [(C_K, 0), (C_Q0, 0), (C_Q1, 0), (C_K, 1), (C_Q0, 1), (C_Q1, 1)]

    with ExitStack() as ctx:
        const = ctx.enter_context(tc.tile_pool(name="const", bufs=1))
        keep = ctx.enter_context(tc.tile_pool(name="keep", bufs=1))
        io = ctx.enter_context(tc.tile_pool(name="io", bufs=3))
        work = ctx.enter_context(tc.tile_pool(name="work", bufs=2))
        psum = ctx.enter_context(tc.psum_pool(name="psum", bufs=1))
        ctx.enter_context(tc.manual_schedule())

        def token_view(rows, g, c0, width):
            return rows[g * 512 : (g + 1) * 512, c0 : c0 + width].rearrange("(p j) w -> p j w", j=PACK)

        u_t, g_t, raw_t = {}, {}, {}

        def load_u(e, split=False):
            c, g = units[e]
            u = io.tile([P, PACK, CH], F32, name="u", bufs=3)
            view = token_view(u2[c], g, first_col[c], CH)
            if split:
                for j in (0, 2):
                    nc.sync.dma_start(out=u[:, j : j + 2, :], in_=view[:, j : j + 2, :])
            else:
                nc.sync.dma_start(out=u[:], in_=view)
            u_t[e] = u

        def load_g(c, g):
            t = io.tile([P, PACK, CH], BF16, name="gr", bufs=4)
            nc.sync.dma_start(out=t[:], in_=token_view(g2[c], g, first_col[c], CH))
            g_t[c, g] = t

        def load_raw(key, rows):
            t = io.tile([P, PACK, DIM], BF16, name="raw", bufs=3)
            nc.sync.dma_start(out=t[:], in_=rows.rearrange("(p j) w -> p j w", j=PACK))
            raw_t[key] = t

        ident_f = const.tile([P, P], F32, name="ident_f")
        make_identity(nc, ident_f[:])
        ident_b = const.tile([P, P], BF16, name="ident_b")
        make_identity(nc, ident_b[:])
        cos_b = const.tile([P, PACK, HALF], BF16, name="cos_b")
        sin_b = const.tile([P, PACK, HALF], BF16, name="sin_b")
        gain_b = const.tile([P, 8], BF16, name="gain_b")
        cos2 = const.tile([P, PACK, 2 * HALF], F32, name="cos2")
        nsin = const.tile([P, PACK, HALF], F32, name="nsin")
        vjunk = const.tile([P, 2, HD], BF16, name="vjunk")
        sel = const.tile([P, 16], F32, name="sel")
        nc.vector.tensor_reduce(out=sel[:], in_=ident_f[:].rearrange("p (g q) -> p g q", q=8), axis=mybir.AxisListType.X, op=ALU.add)
        sjunk = const.tile([P, 8, HD], BF16, name="sjunk")

        load_u(0, split=True)
        load_g(*units[0])
        for half in range(2):
            rows = slice(64 * half, 64 * half + 64)
            nc.sync.dma_start(out=cos_b[rows], in_=cos_tab.rearrange("(p j) w -> p j w", j=PACK))
            nc.sync.dma_start(out=sin_b[rows], in_=sin_tab.rearrange("(p j) w -> p j w", j=PACK))
        nc.sync.dma_start(out=gain_b[:], in_=q_gain.partition_broadcast(P))
        load_g(C_V, 0)
        load_u(1)
        load_g(*units[1])
        load_g(C_V, 1)
        load_raw("x0", x2[0:512, :])
        load_raw("x1", x2[512:1024, :])
        dz_t = {(C_V, 0): g_t[C_V, 0], (C_V, 1): g_t[C_V, 1]}
        def tables():
            nc.scalar.copy(out=cos2[:, :, 0:HALF], in_=cos_b[:])
            nc.scalar.copy(out=cos2[:, :, HALF : 2 * HALF], in_=cos_b[:])
            nc.gpsimd.tensor_scalar(out=nsin[:], in0=sin_b[:], scalar1=-1.0, scalar2=0.0, op0=ALU.mult, op1=ALU.add)

        zf_codes = keep.tile([P, 8, CH], U32, name="zf_codes", align_bytes=64)
        zf_scales = keep.tile([P, 8, CH], U8, name="zf_scales", align_bytes=64)
        x_codes = keep.tile([P, 2, DIM], U32, name="x_codes", align_bytes=64)
        x_scales = keep.tile([P, 2, DIM], U8, name="x_scales", align_bytes=64)
        w_codes = keep.tile([P, 4, DIM], U32, name="w_codes", align_bytes=64)
        w_scales = keep.tile([P, 4, DIM], U8, name="w_scales", align_bytes=64)
        zt = {}

        def bank(i, shape, dtype):
            return psum.tile(shape, dtype, name="bank%d" % i, tag="bank%d" % i)

        ss_t, std_t, r_t, a_t, nr_t, d_t, y_t, nb_t = {}, {}, {}, {}, {}, {}, {}, {}

        def squares(e, on_vector=()):
            ss = work.tile([P, 16], F32, name="ss", bufs=2)
            for j in range(PACK):
                for h in range(HEADS):
                    i = j * HEADS + h
                    src = u_t[e][:, j, h * HD : (h + 1) * HD]
                    if j in on_vector:
                        nc.vector.scalar_tensor_tensor(out=vjunk[:, i % 2, :], in0=src, scalar=1.0, in1=src,
                                                       op0=ALU.mult, op1=ALU.mult, accum_out=ss[:, i : i + 1])
                    else:
                        nc.scalar.activation(out=sjunk[:, i % 8, :], in_=src, func=ACT.Square, accum_out=ss[:, i : i + 1])
            ss_t[e] = ss

        def root(e):
            std = work.tile([P, 16], F32, name="std", bufs=2)
            nc.scalar.activation(out=std[:], in_=ss_t[e][:], func=ACT.Sqrt, scale=1.0 / HD, bias=EPS)
            std_t[e] = std

        def inverse(e):
            r = work.tile([P, 16], F32, name="r", bufs=3)
            nc.vector.reciprocal(out=r[:], in_=std_t[e][:])
            r_t[e] = r

        def factors(e):
            c, g = units[e]
            r = r_t[e]
            if c == C_K:
                a_t[e] = r
            else:
                a = work.tile([P, 16], F32, name="a", bufs=3)
                h0 = HEADS * c
                nc.vector.tensor_tensor(
                    out=a[:].rearrange("p (j h) -> p j h", h=HEADS), in0=r[:].rearrange("p (j h) -> p j h", h=HEADS),
                    in1=gain_b[:, h0 : h0 + HEADS].unsqueeze(1).to_broadcast([P, PACK, HEADS]), op=ALU.mult)
                a_t[e] = a
            nr = work.tile([P, 16], F32, name="nr", bufs=3)
            nc.vector.scalar_tensor_tensor(out=nr[:], in0=r[:], scalar=-1.0 / HD, in1=r[:], op0=ALU.mult, op1=ALU.mult)
            nr_t[e] = nr

        def scale(e, slots=range(PACK), on_vector=()):
            if e not in d_t:
                d_t[e] = work.tile([P, PACK, CH], F32, name="d", bufs=2)
            for j in slots:
                for h in range(HEADS):
                    i = j * HEADS + h
                    cols = slice(h * HD, (h + 1) * HD)
                    if j in on_vector:
                        nc.vector.tensor_scalar(out=d_t[e][:, j, cols], in0=g_t[units[e]][:, j, cols],
                                                scalar1=a_t[e][:, i : i + 1], scalar2=None, op0=ALU.mult)
                    else:
                        nc.scalar.activation(out=d_t[e][:, j, cols], in_=g_t[units[e]][:, j, cols], func=ACT.Copy,
                                             scale=a_t[e][:, i : i + 1])

        def heads(d):
            return d[:].rearrange("p j (h f) -> p j h f", f=HD)

        def rotate_products(e, j0=0, j1=PACK):
            d = heads(d_t[e])[:, j0:j1]
            if e not in y_t:
                y_t[e] = work.tile([P, PACK, HEADS, 2 * HALF], F32, name="y", bufs=1)
            y = y_t[e][:, j0:j1]
            full = [P, j1 - j0, HEADS, HALF]
            nc.vector.tensor_tensor(out=y[:, :, :, 0:HALF], in0=d[:, :, :, HALF : 2 * HALF],
                                    in1=nsin[:, j0:j1].unsqueeze(2).to_broadcast(full), op=ALU.mult)
            nc.vector.tensor_tensor(out=y[:, :, :, HALF : 2 * HALF], in0=d[:, :, :, 0:HALF],
                                    in1=sin_b[:, j0:j1].unsqueeze(2).to_broadcast(full), op=ALU.mult)
            nc.vector.tensor_tensor(out=d[:, :, :, 0 : 2 * HALF], in0=d[:, :, :, 0 : 2 * HALF],
                                    in1=cos2[:, j0:j1].unsqueeze(2).to_broadcast([P, j1 - j0, HEADS, 2 * HALF]), op=ALU.mult)

        def rotate_sum(e, j0=0, j1=PACK):
            d = heads(d_t[e])[:, j0:j1, :, 0 : 2 * HALF]
            nc.vector.tensor_tensor(out=d, in0=d, in1=y_t[e][:, j0:j1], op=ALU.add)

        prod_t, dot_t, pt_t = {}, {}, {}

        def products(e, half):
            if e not in prod_t:
                prod_t[e] = work.tile([P, 16, P], F32, name="prod", bufs=1)
            s = slice(8 * half, 8 * half + 8)
            nc.vector.tensor_tensor(out=prod_t[e][:, s, :].rearrange("p s (g q) -> p g s q", q=8),
                                    in0=d_t[e][:].rearrange("p j (h b q) -> p (j h) b q", b=16, q=8)[:, :, s, :],
                                    in1=u_t[e][:].rearrange("p j (h b q) -> p (j h) b q", b=16, q=8)[:, :, s, :], op=ALU.mult)

        def dot_transposes(e, half):
            if half == 1:
                dot_t[e] = bank(0, [P, 512], F32)
            for k in range(8 * half, 8 * half + 8):
                nc.tensor.matmul(dot_t[e][:, 0:P], prod_t[e][:, k, :], ident_f[:], is_transpose=True,
                                 start=(k == 8), stop=(k == 7))

        def dot_copy(e):
            pt_t[e] = work.tile([P, P], F32, name="pt", bufs=2)
            nc.scalar.copy(out=pt_t[e][:], in_=dot_t[e][:, 0:P])
            nc.tensor.matmul(dot_t[e][:, P : P + 16], pt_t[e][:], sel[:], start=True, stop=True)

        def dot_finish(e):
            nb_t[e] = work.tile([P, 16], F32, name="nb", bufs=2)
            nc.vector.tensor_tensor(out=nb_t[e][:], in0=dot_t[e][:, P : P + 16], in1=nr_t[e][:], op=ALU.mult)

        def finish(e, slots=range(PACK)):
            key = units[e]
            if key not in dz_t:
                dz_t[key] = work.tile([P, PACK, CH], BF16, name="dz", bufs=2)
            for j in slots:
                for h in range(HEADS):
                    i = j * HEADS + h
                    cols = slice(h * HD, (h + 1) * HD)
                    nc.vector.scalar_tensor_tensor(
                        out=dz_t[key][:, j, cols], in0=u_t[e][:, j, cols], scalar=nb_t[e][:, i : i + 1],
                        in1=d_t[e][:, j, cols], op0=ALU.mult, op1=ALU.add)

        zi_t, zf_t, zt, xt_t = {}, {}, {}, {}

        def token_interleave(key, c0, c1, engine="v"):
            if c1 == c0:
                return
            if key not in zi_t:
                zi_t[key] = work.tile([P, CH, PACK], BF16, name="zi", align_bytes=64, bufs=2)
            dst = zi_t[key][:, c0:c1, :].rearrange("p (c i) t -> p c t i", i=4)
            src = dz_t[key][:, :, c0:c1].rearrange("p t (c i) -> p c t i", i=4)
            if engine == "s":
                nc.scalar.copy(out=dst, in_=src)
            else:
                nc.vector.tensor_copy(out=dst, in_=src)

        def token_quantize(key, c0=0, c1=CH):
            if key not in zt:
                zt[key] = (work.tile([P, CH], U32, name="zt_codes", align_bytes=64, bufs=6),
                           work.tile([P, CH], U8, name="zt_scales", align_bytes=64, bufs=6))
            codes, scales = zt[key]
            nc.vector.quantize_mx(out=codes[:, c0:c1].bitcast(E5M2), scales=scales[:, c0:c1],
                                  in_=zi_t[key][:, c0:c1, :].rearrange("p n t -> p (n t)"))

        def transposes(key, slots=range(PACK)):
            words = dz_t[key][:].rearrange("p j f -> p (j f)").bitcast(F32)
            for j in slots:
                if j % 2 == 0:
                    xt_t[key, j // 2] = bank(j // 2, [P, 2, 2, P], F32)
                for u in range(2):
                    nc.tensor.transpose(xt_t[key, j // 2][:, j % 2, u, :],
                                        words[:, 256 * j + u : 256 * (j + 1) : 2], ident_f[:])

        def feature_copy(key, slots=range(PACK)):
            if key not in zf_t:
                zf_t[key] = work.tile([P, CH, PACK], BF16, name="zf", align_bytes=64, bufs=2)
            zfw = zf_t[key][:].rearrange("p n t -> p (n t)").bitcast(F32).rearrange("p (j r u) -> p j r u", j=PACK, u=2)
            for b in range(2):
                js = [j for j in slots if j // 2 == b]
                if js:
                    nc.scalar.copy(out=zfw[:, js[0] : js[-1] + 1, :, :],
                                   in_=xt_t[key, b][:, js[0] - 2 * b : js[-1] + 1 - 2 * b].rearrange("p j u r -> p j r u"))

        def feature_quantize(key, j0=0, j1=PACK):
            c, g = key
            s = 4 * g + c
            cols = slice(P * j0, P * j1)
            nc.vector.quantize_mx(out=zf_codes[:, s, cols].bitcast(E5M2), scales=zf_scales[:, s, cols],
                                  in_=zf_t[key][:, cols, :].rearrange("p n t -> p (n t)"))

        xi_t, ps_t = {}, {}
        ring = [2]

        def next_bank():
            b = ring[0]
            ring[0] = b + 1 if b < 7 else 2
            return b

        def raw_mm(key, i):
            ps = bank(next_bank(), [P, 1024], BF16)
            ps_t[key, i] = ps
            for hh in range(2):
                w0 = 256 * i + 128 * hh
                nc.tensor.matmul(ps[:, 512 * hh : 512 * (hh + 1)].rearrange("p (w j) -> p w j", j=PACK), ident_b[:],
                                 raw_t[key][:, :, w0 : w0 + 128].rearrange("p j w -> p w j"), start=True, stop=True)

        def raw_copy(key, i):
            if (key, i // 2) not in xi_t:
                xi_t[key, i // 2] = work.tile([P, 2048], BF16, name="xi", align_bytes=64, bufs=4)
            nc.scalar.copy(out=xi_t[key, i // 2][:, 1024 * (i % 2) : 1024 * (i % 2 + 1)], in_=ps_t[key, i][:])

        def raw_quantize(key, half):
            codes, scales = (x_codes, x_scales) if key[0] == "x" else (w_codes, w_scales)
            s = int(key[1])
            cols = slice(512 * half, 512 * half + 512)
            nc.vector.quantize_mx(out=codes[:, s, cols].bitcast(E4M3), scales=scales[:, s, cols], in_=xi_t[key, half][:])

        def evacuate(acc, dst, engine):
            if engine == "s":
                nc.scalar.copy(out=dst, in_=acc)
            else:
                nc.vector.tensor_copy(out=dst, in_=acc)

        def weight_mm(c, m, n, g, acc):
            codes, scales = zt[c, g]
            nc.tensor.matmul_mx(out=acc[:], lhsT=codes[:, m * P : (m + 1) * P].bitcast(E5M2),
                                lhsT_scale=scales[:, m * P : (m + 1) * P],
                                rhs=x_codes[:, g, 512 * n : 512 * (n + 1)].bitcast(E4M3),
                                rhs_scale=x_scales[:, g, 512 * n : 512 * (n + 1)], start=(g == 0), stop=(g == 1))

        def weight_open(c, m, banks=None, passes=(0, 1)):
            for n in range(2):
                if (c, m, n) not in wacc_t:
                    wacc_t[c, m, n] = bank(banks[n] if banks else next_bank(), [P, 512], F32)
                for g in passes:
                    weight_mm(c, m, n, g, wacc_t[c, m, n])

        o_t = {}

        def emit(key, n, acc, rows, engine):
            if key not in o_t:
                o_t[key] = io.tile([P, DIM], F32, name="o", bufs=6)
            evacuate(acc[:], o_t[key][:, 512 * n : 512 * (n + 1)], engine)
            if n == 1:
                nc.sync.dma_start(out=rows, in_=o_t[key][:])

        def weight_out(c, m, n, engine="s"):
            emit((c, m), n, wacc_t[c, m, n], dw_rows[c][m * P : (m + 1) * P, :], engine)

        def data_out(g, j, n, engine="s"):
            emit(("x", g, j), n, acc_t[g, j, n], token_view(dx2, g, 0, DIM)[:, j, :], engine)

        order = [C_V, C_K, C_Q0, C_Q1]
        acc_t, wacc_t = {}, {}

        def data_mm(g, j, n, passes):
            for i in passes:
                c = order[i]
                s = 4 * g + c
                nc.tensor.matmul_mx(out=acc_t[g, j, n][:], lhsT=zf_codes[:, s, j * P : (j + 1) * P].bitcast(E5M2),
                                    lhsT_scale=zf_scales[:, s, j * P : (j + 1) * P],
                                    rhs=w_codes[:, c, 512 * n : 512 * (n + 1)].bitcast(E4M3),
                                    rhs_scale=w_scales[:, c, 512 * n : 512 * (n + 1)],
                                    start=(i == 0), stop=(i == 3))

        def data_open(g, j, banks, passes):
            for n in range(2):
                acc_t[g, j, n] = bank(banks[n] if banks else next_bank(), [P, 512], F32)
                data_mm(g, j, n, passes)

        V0, V1 = (C_V, 0), (C_V, 1)
        squares(0, on_vector=(2, 3))
        root(0)
        transposes(V0)
        inverse(0)
        factors(0)
        scale(0, [0, 1], on_vector=(0, 1))
        tables()
        scale(0, [2, 3])
        load_u(2)
        load_g(*units[2])
        load_raw("w3", w_rows[C_V])
        rotate_products(0, 0, 2)
        token_interleave(V0, 0, CH)
        rotate_sum(0, 0, 2)
        rotate_products(0, 2, 4)
        token_quantize(V0)
        rotate_sum(0, 2, 4)
        feature_copy(V0)
        squares(1)
        root(1)
        transposes(V1)
        feature_copy(V1)
        raw_mm("x0", 0)
        raw_mm("x0", 1)
        inverse(1)
        products(0, 1)
        factors(1)
        dot_transposes(0, 1)
        products(0, 0)
        dot_transposes(0, 0)
        scale(1)
        feature_quantize(V0)
        token_interleave(V1, 0, CH)
        dot_copy(0)
        raw_mm("x0", 2)
        raw_mm("x0", 3)
        for i in range(4):
            raw_copy("x0", i)
        raw_mm("x1", 0)
        raw_mm("x1", 1)
        token_quantize(V1)
        feature_quantize(V1)
        dot_finish(0)

        loads = {
            1: lambda: (load_raw("w2", w_rows[C_K]), load_u(3), load_g(*units[3]), load_raw("w0", w_rows[C_Q0])),
            2: lambda: (load_raw("w1", w_rows[C_Q1]), load_u(4), load_g(*units[4])),
            3: lambda: (load_u(5), load_g(*units[5])),
        }

        def wo(c, m):
            return lambda: weight_open(c, m)

        def do(g, j):
            return lambda: data_open(g, j, None, range(4))

        def we(c, m, n):
            return lambda: weight_out(c, m, n)

        def de(g, j, n):
            return lambda: data_out(g, j, n)

        def rm(key, *tiles):
            return lambda: [raw_mm(key, i) for i in tiles]

        def rc(key, *tiles):
            return lambda: [raw_copy(key, i) for i in tiles]

        def rq(key, half):
            return lambda: raw_quantize(key, half)

        def run(fs):
            for f in fs:
                f()

        def step(e, pe0=(), pe1=(), pe2=(), pe3=(), s0=(), s1=(), s2=(), v0=(), v1=(), s_cols=0):
            prev = units[e - 1]
            run(pe0)
            finish(e - 1)
            squares(e + 1)
            root(e + 1)
            run(s0)
            transposes(prev)
            run(pe1)
            if e in loads:
                loads[e]()
            rotate_products(e)
            products(e, 1)
            feature_copy(prev)
            token_interleave(prev, 0, s_cols, "s")
            run(s1)
            dot_transposes(e, 1)
            run(pe2)
            rotate_sum(e)
            inverse(e + 1)
            run(v0)
            token_interleave(prev, s_cols, CH)
            factors(e + 1)
            products(e, 0)
            dot_transposes(e, 0)
            scale(e + 1)
            feature_quantize(prev)
            dot_copy(e)
            token_quantize(prev)
            run(v1)
            run(s2)
            run(pe3)
            dot_finish(e)

        step(1, pe0=[rm("x1", 2, 3)], pe1=[rm("w3", 0, 1)], pe2=[rm("w3", 2, 3)], pe3=[rm("w2", 0, 1)],
             s0=[rc("x1", 0)], s1=[rc("x1", 1, 2, 3)], s2=[rc("w3", 0, 1, 2, 3)],
             v0=[rq("x0", 0), rq("x0", 1)], v1=[rq("x1", 0), rq("x1", 1)], s_cols=128)
        step(2, pe0=[rm("w2", 2, 3)], pe1=[rm("w0", 0, 1)], pe2=[rm("w0", 2, 3), wo(C_V, 0)], pe3=[wo(C_V, 1), rm("w1", 0, 1)],
             s0=[rc("w2", 0)], s1=[rc("w2", 1, 2, 3)], s2=[rc("w0", 0, 1), we(C_V, 0, 0), we(C_V, 0, 1), rc("w0", 2, 3)],
             v0=[rq("w3", 0), rq("w3", 1)], v1=[rq("w2", 0), rq("w2", 1)], s_cols=64)
        step(3, pe0=[rm("w1", 2, 3)], pe1=[wo(C_V, 2)], pe2=[wo(C_V, 3)], pe3=[do(0, 0)],
             s0=[we(C_V, 1, 0), we(C_V, 1, 1)], s1=[rc("w1", 0, 1, 2, 3)], s2=[we(C_V, 2, 0), we(C_V, 2, 1), we(C_V, 3, 0), we(C_V, 3, 1)],
             v0=[rq("w0", 0), rq("w0", 1)], v1=[rq("w1", 0), rq("w1", 1)], s_cols=0)
        step(4, pe0=[do(0, 1)], pe1=[do(0, 2)], pe2=[do(0, 3)], pe3=[wo(C_K, 0)],
             s0=[de(0, 0, 0)], s1=[de(0, 0, 1), de(0, 1, 0), de(0, 1, 1)], s2=[de(0, 2, 0), de(0, 2, 1), de(0, 3, 0), de(0, 3, 1)], s_cols=128)

        last = units[5]
        prev = units[4]
        finish(4)
        transposes(prev)
        wo(C_K, 1)()
        token_interleave(prev, 0, 192, "s")
        token_interleave(prev, 192, CH)
        run([we(C_K, 0, 0), we(C_K, 0, 1)])
        feature_copy(prev)
        rotate_products(5)
        token_quantize(prev)
        wo(C_K, 2)()
        products(5, 1)
        run([we(C_K, 1, 0), we(C_K, 1, 1)])
        dot_transposes(5, 1)
        wo(C_K, 3)()
        rotate_sum(5)
        run([we(C_K, 2, 0), we(C_K, 2, 1)])
        feature_quantize(prev)
        wo(C_Q0, 0)()
        products(5, 0)
        dot_transposes(5, 0)
        run([we(C_K, 3, 0)])
        dot_copy(5)
        weight_out(C_K, 3, 1, "v")
        wo(C_Q0, 1)()
        run([we(C_Q0, 0, 0)])
        weight_out(C_Q0, 0, 1, "v")
        wo(C_Q0, 2)()
        dot_finish(5)
        finish(5, [0])
        run([we(C_Q0, 1, 0), we(C_Q0, 1, 1)])
        wo(C_Q0, 3)()
        transposes(last, [0])
        finish(5, [1])
        run([we(C_Q0, 2, 0)])
        feature_copy(last, [0])
        run([we(C_Q0, 2, 1)])
        data_open(1, 0, None, range(3))
        transposes(last, [1])
        feature_quantize(last, 0, 1)
        finish(5, [2])
        feature_copy(last, [1])
        run([we(C_Q0, 3, 0), we(C_Q0, 3, 1)])
        data_open(1, 1, None, range(3))
        transposes(last, [2])
        finish(5, [3])
        data_mm(1, 0, 0, [3])
        data_mm(1, 0, 1, [3])
        feature_copy(last, [2])
        feature_quantize(last, 1, 2)
        transposes(last, [3])
        data_mm(1, 1, 0, [3])
        data_mm(1, 1, 1, [3])
        run([de(1, 0, 0), de(1, 0, 1)])
        feature_copy(last, [3])
        token_interleave(last, 0, 256)
        feature_quantize(last, 2, 3)
        data_open(1, 2, None, range(4))
        token_interleave(last, 256, CH)
        run([de(1, 1, 0), de(1, 1, 1)])
        feature_quantize(last, 3, 4)
        token_quantize(last, 0, 256)
        token_quantize(last, 256, CH)
        do(1, 3)()
        run([de(1, 2, 0)])
        data_out(1, 2, 1, "v")
        wo(C_Q1, 0)()
        run([de(1, 3, 0)])
        data_out(1, 3, 1, "v")
        for m in range(4):
            if m < 3:
                wo(C_Q1, m + 1)()
            weight_out(C_Q1, m, 0, "s")
            weight_out(C_Q1, m, 1, "v")
